import numpy as np
import ml_dtypes


def mxq(x, axis, fmt="e4m3"):
    dtype, down = {"e4m3": (ml_dtypes.float8_e4m3fn, 7), "e5m2": (ml_dtypes.float8_e5m2, 14)}[fmt]
    v = np.moveaxis(np.asarray(x, np.float32).astype(ml_dtypes.bfloat16).astype(np.float64), axis, -1)
    blocks = v.reshape(v.shape[:-1] + (-1, 32))
    amax = np.abs(blocks).max(-1, keepdims=True)
    byte = np.maximum(np.where(amax > 0, np.frexp(amax)[1] - 1 + 127, 0) - down, 1)
    scale = np.exp2(byte - 127.0)
    codes = (blocks / scale).astype(np.float32).astype(dtype).astype(np.float64)
    return np.moveaxis((codes * scale).reshape(v.shape), -1, axis)


WIDE = False


def mx_kscale(k):
    if not WIDE:
        return np.ones(k)
    levels = np.array([10, -10, 5, -5, 0])
    if k % 512:
        return np.exp2(np.random.permutation(np.resize(levels, k // 32))).repeat(32)
    a = np.empty((k // 512, 16))
    for p in range(k // 512):
        a[p, :8] = np.random.permutation(np.resize(levels, 8))
        for g in range(8):
            far = levels[np.abs(levels - a[p, g]) >= 10]
            a[p, g + 8] = far[np.random.randint(len(far))]
    return np.exp2(a.ravel()).repeat(32)


BF16 = ml_dtypes.bfloat16


def bf(x):
    return np.asarray(x, np.float32).astype(BF16)


def f64(x):
    return np.asarray(x).astype(np.float64)


B, G, DB, DR = 128, 16, 1024, 2048


def mish(v):
    return v * np.tanh(np.log(1.0 + np.exp(v)))


def setup_inputs():
    s, t = mx_kscale(DR), mx_kscale(DB)
    return {"BB_feature": bf(np.random.standard_normal((B, G, DB)) * t),
            "RF_feature": bf(np.random.standard_normal((B, DR)) * s),
            "W_rfrf": bf(np.random.standard_normal((DR, DR)) / np.sqrt(DR) / s),
            "b_rfrf": bf(np.random.standard_normal(DR) * 0.5),
            "W_bbrf": bf(np.random.standard_normal((DR, DB)) * np.sqrt(G / DB) / t),
            "b_bbrf": bf(np.random.standard_normal(DR) * 0.5)}


def reference(BB_feature, RF_feature, W_rfrf, b_rfrf, W_bbrf, b_bbrf):
    BB_mean = np.mean(f64(BB_feature), axis=-2)
    RF_to_RF = mish((mxq(f64(RF_feature), 1, "e4m3") @ mxq(f64(W_rfrf), 1, "e4m3").T) + f64(b_rfrf))
    BB_to_RF = mish((mxq(BB_mean, 1, "e4m3") @ mxq(f64(W_bbrf), 1, "e4m3").T) + f64(b_bbrf))
    return RF_to_RF + BB_to_RF

@@ -1,0 +1,235 @@
+import concourse.mybir as mybir
+from concourse.masks import make_identity
+
+F32 = mybir.dt.float32
+BF16 = mybir.dt.bfloat16
+U32 = mybir.dt.uint32
+U8 = mybir.dt.uint8
+FP8X4 = mybir.dt.float8_e4m3fn_x4
+ACT = mybir.ActivationFunctionType
+ALU = mybir.AluOpType
+
+P = 128
+GROUPS = 16
+D_BB = 1024
+D_RF = 2048
+K_PASS = 512
+ROWS = 2
+WIDTH = P * ROWS
+SLOTS_PER_LAYER = D_RF // WIDTH
+SLOTS = 2 * SLOTS_PER_LAYER
+FIRST_BATCH = 11
+EXP_CAP = 30.0
+
+FLOPS = 2 * P * D_RF * (D_RF + D_BB)
+
+
+def tile_gnn_layer_pa_kernel(tc, BB_feature, RF_feature, W_rfrf, b_rfrf, W_bbrf, b_bbrf, out):
+    nc = tc.nc
+    with (
+        tc.tile_pool(name="const", bufs=1) as const,
+        tc.tile_pool(name="work", bufs=2) as work,
+        tc.psum_pool(name="tp", bufs=4) as tp,
+        tc.psum_pool(name="accp", bufs=2) as accp,
+        tc.psum_pool(name="meanp", bufs=1) as meanp,
+        tc.manual_schedule(),
+    ):
+        bias_rows = const.tile([P, P], BF16)
+        nc.vector.memset(bias_rows[:], 0.0)
+        nc.sync.dma_start(out=bias_rows[0:16, :], in_=b_rfrf.rearrange("(r c) -> r c", c=P))
+        nc.sync.dma_start(out=bias_rows[16:32, :], in_=b_bbrf.rearrange("(r c) -> r c", c=P))
+
+        rf_raw = const.tile([P, D_RF], BF16)
+        nc.sync.dma_start(out=rf_raw[:], in_=RF_feature)
+
+        def load_weight_slot(w, k, index):
+            w_raw = const.tile([P, ROWS * k], BF16, name="w_raw_%d_%d" % (k, index))
+            nc.sync.dma_start(
+                out=w_raw[:],
+                in_=w[index * WIDTH : (index + 1) * WIDTH, :].rearrange("(n j) k -> n (j k)", j=ROWS),
+            )
+            return w_raw
+
+        bb_rows = BB_feature.rearrange("b g d -> (b g) d")
+        w_raw_tiles = []
+        bb_raw_tiles = []
+        for i in range(4):
+            w_raw_tiles.append(load_weight_slot(W_rfrf, D_RF, 2 * i))
+            w_raw_tiles.append(load_weight_slot(W_rfrf, D_RF, 2 * i + 1))
+            bb_raw = const.tile([P, 4 * D_BB], BF16, name="bb_raw_%d" % i)
+            nc.sync.dma_start(
+                out=bb_raw[:],
+                in_=bb_rows[i * 512 : (i + 1) * 512, :].rearrange("(p e) d -> p (e d)", e=4),
+            )
+            bb_raw_tiles.append(bb_raw)
+        w_raw_tiles.extend([load_weight_slot(W_bbrf, D_BB, i) for i in range(SLOTS_PER_LAYER)])
+
+        ident = const.tile([P, P], F32)
+        make_identity(nc, ident[:])
+        sel_f32 = const.tile([P, 32], F32)
+        nc.vector.tensor_reduce(
+            out=sel_f32[:],
+            in_=ident[:].rearrange("p (n i) -> p n i", i=4),
+            axis=mybir.AxisListType.X,
+            op=ALU.add,
+        )
+        sel = const.tile([P, 32], BF16)
+        nc.vector.tensor_scalar(out=sel[:], in0=sel_f32[:], scalar1=1.0 / GROUPS, scalar2=None, op0=ALU.mult)
+
+        def transpose_and_group(src, rows, k, grouped, vector_banks):
+            words = src[:].bitcast(F32)
+            grouped_words = grouped.bitcast(F32).rearrange("p (g n u) -> p g n u", n=P, u=2)
+            n_groups = rows * (k // K_PASS)
+            for pair in range(n_groups // 2):
+                bank = tp.tile([P, 512], F32, tag="tp", name="bank")
+                bank_v = bank[:].rearrange("p (h u n) -> p h u n", h=2, u=2)
+                for h in range(2):
+                    c, j = divmod(2 * pair + h, rows)
+                    for u in range(2):
+                        first = j * (k // 2) + 256 * c
+                        nc.tensor.transpose(bank_v[:, h, u, :], words[:, first + u : first + 256 : 2], ident[:])
+                copy = nc.vector.tensor_copy if pair < vector_banks else nc.scalar.copy
+                copy(
+                    out=grouped_words[:, 2 * pair : 2 * pair + 2, :, :],
+                    in_=bank[:].rearrange("p (h u n) -> p h n u", h=2, u=2),
+                )
+
+        def depth_of(slot):
+            return D_RF if slot < SLOTS_PER_LAYER else D_BB
+
+        def transpose_slot(slot):
+            k = depth_of(slot)
+            grouped = work.tile([P, ROWS * D_RF], BF16, align_bytes=64, tag="grouped", name="grouped", bufs=3)
+            if slot >= FIRST_BATCH + 3:
+                vector_banks = 4
+            elif slot < SLOTS_PER_LAYER:
+                vector_banks = 1
+            else:
+                vector_banks = slot % 2
+            transpose_and_group(w_raw_tiles[slot], ROWS, k, grouped[:, : ROWS * k], vector_banks)
+            return grouped
+
+        def quantise_slot(slot, grouped):
+            k = depth_of(slot)
+            codes = work.tile([P, ROWS * D_RF // 4], U32, align_bytes=64, tag="codes", name="codes")
+            scales = work.tile([P, ROWS * D_RF // 4], U8, align_bytes=64, tag="scales", name="scales")
+            n_words = ROWS * k // 4
+            nc.vector.quantize_mx(
+                out=codes[:, :n_words].bitcast(FP8X4), scales=scales[:, :n_words], in_=grouped[:, : ROWS * k]
+            )
+            return codes, scales
+
+        z = const.tile([P, 2 * D_RF], F32)
+        soft = const.tile([P, 2 * D_RF], F32)
+        x_grouped = [const.tile([P, k], BF16, align_bytes=64, name="x_grouped_%d" % k) for k in (D_RF, D_BB)]
+        x_codes = [const.tile([P, k // 4], U32, align_bytes=64, name="x_codes_%d" % k) for k in (D_RF, D_BB)]
+        x_scales = [const.tile([P, k // 4], U8, align_bytes=64, name="x_scales_%d" % k) for k in (D_RF, D_BB)]
+        bias = const.tile([P, 2 * D_RF], F32)
+        mean_banks = [meanp.tile([P, 512], F32, tag="mean%d" % c, name="mean%d" % c) for c in range(2)]
+
+        def quantise_x(layer):
+            nc.vector.quantize_mx(
+                out=x_codes[layer][:].bitcast(FP8X4), scales=x_scales[layer][:], in_=x_grouped[layer][:]
+            )
+
+        def spread_biases():
+            rows_f32 = const.tile([P, P], F32)
+            nc.vector.tensor_copy(out=rows_f32[:], in_=bias_rows[:])
+            columns_bank = tp.tile([P, 512], F32, tag="tp", name="columns_bank")
+            nc.tensor.transpose(columns_bank[:, :P], rows_f32[:], ident[:])
+            columns = const.tile([P, 32], F32)
+            nc.vector.tensor_copy(out=columns[:], in_=columns_bank[:, :32])
+            for index in range(8):
+                bank = tp.tile([P, 512], F32, tag="tp", name="bias_bank")
+                for quarter in range(4):
+                    r = 4 * index + quarter
+                    nc.tensor.transpose(
+                        bank[:, quarter * P : (quarter + 1) * P], columns[:, r : r + 1].to_broadcast([P, P]), ident[:]
+                    )
+                copy = nc.vector.tensor_copy if index % 2 == 0 else nc.scalar.copy
+                copy(out=bias[:, index * 512 : (index + 1) * 512], in_=bank[:])
+
+        def multiply_slot(slot, w_codes, w_scales):
+            layer = slot // SLOTS_PER_LAYER
+            passes = depth_of(slot) // K_PASS
+            acc = accp.tile([P, WIDTH], F32, tag="acc", name="acc")
+            for c in range(passes):
+                nc.tensor.matmul_mx(
+                    out=acc[:],
+                    lhsT=x_codes[layer][:, c * P : (c + 1) * P].bitcast(FP8X4),
+                    lhsT_scale=x_scales[layer][:, c * P : (c + 1) * P],
+                    rhs=w_codes[:, c * WIDTH : (c + 1) * WIDTH].bitcast(FP8X4),
+                    rhs_scale=w_scales[:, c * WIDTH : (c + 1) * WIDTH],
+                    start=(c == 0),
+                    stop=(c == passes - 1),
+                )
+            return acc
+
+        def add_bias_and_exp(slot, acc):
+            cols = slice(slot * WIDTH, (slot + 1) * WIDTH)
+            nc.vector.tensor_tensor(
+                out=z[:, cols].rearrange("p (n j) -> p n j", j=ROWS),
+                in0=acc[:].rearrange("p (j n) -> p n j", j=ROWS),
+                in1=bias[:, cols].rearrange("p (n j) -> p n j", j=ROWS),
+                op=ALU.add,
+            )
+            nc.vector.tensor_scalar(out=soft[:, cols], in0=z[:, cols], scalar1=EXP_CAP, scalar2=None, op0=ALU.min)
+            nc.scalar.activation(out=soft[:, cols], in_=soft[:, cols], func=ACT.Exp)
+
+        def mean_part(index):
+            i, c = divmod(index, 2)
+            bb_v = bb_raw_tiles[i][:].rearrange("p (e c q t) -> p e c t q", e=4, c=2, t=4)
+            mean_v = mean_banks[c][:].rearrange("p (t b) -> p t b", t=4)
+            for t in range(4):
+                for e in range(4):
+                    nc.tensor.matmul(
+                        out=mean_v[:, t, 32 * i : 32 * i + 32],
+                        lhsT=bb_v[:, e, c, t, :],
+                        rhs=sel[:],
+                        start=(e == 0),
+                        stop=(e == 3),
+                    )
+
+        transpose_and_group(rf_raw, 1, D_RF, x_grouped[0][:], 1)
+
+        early = slice(0, FIRST_BATCH * WIDTH)
+        late = slice(FIRST_BATCH * WIDTH, SLOTS * WIDTH)
+        grouped = {}
+        codes = {}
+        acc = {}
+        for step in range(-2, SLOTS + 1):
+            if step + 2 < SLOTS:
+                grouped[step + 2] = transpose_slot(step + 2)
+            if step == -2:
+                quantise_x(0)
+            if step == -1:
+                spread_biases()
+            if step >= 1:
+                add_bias_and_exp(step - 1, acc[step - 1])
+            if step == FIRST_BATCH:
+                nc.scalar.activation(out=soft[:, early], in_=soft[:, early], func=ACT.Ln, bias=1.0)
+                nc.scalar.activation(out=soft[:, early], in_=soft[:, early], func=ACT.Tanh)
+            if 0 <= step + 1 < SLOTS:
+                codes[step + 1] = quantise_slot(step + 1, grouped[step + 1])
+            if 0 <= step < SLOTS:
+                acc[step] = multiply_slot(step, codes[step][0], codes[step][1])
+            if 0 <= step < SLOTS_PER_LAYER:
+                mean_part(step)
+            if step == SLOTS_PER_LAYER - 1:
+                for c in range(2):
+                    nc.vector.tensor_copy(
+                        out=x_grouped[1][:, c * 512 : (c + 1) * 512].rearrange("p (b t) -> p b t", t=4),
+                        in_=mean_banks[c][:].rearrange("p (t b) -> p b t", t=4),
+                    )
+                quantise_x(1)
+
+        nc.scalar.activation(out=soft[:, late], in_=soft[:, late], func=ACT.Ln, bias=1.0)
+        nc.vector.tensor_tensor(out=soft[:, early], in0=z[:, early], in1=soft[:, early], op=ALU.mult)
+        for slot in range(SLOTS_PER_LAYER, SLOTS):
+            cols = slice(slot * WIDTH, (slot + 1) * WIDTH)
+            out_cols = slice((slot - SLOTS_PER_LAYER) * WIDTH, (slot - SLOTS_PER_LAYER + 1) * WIDTH)
+            if slot >= FIRST_BATCH:
+                nc.scalar.activation(out=soft[:, cols], in_=soft[:, cols], func=ACT.Tanh)
+                nc.vector.tensor_tensor(out=soft[:, cols], in0=z[:, cols], in1=soft[:, cols], op=ALU.mult)
+            nc.vector.tensor_tensor(out=soft[:, cols], in0=soft[:, cols], in1=soft[:, out_cols], op=ALU.add)
+            nc.sync.dma_start(out=out[:, out_cols], in_=soft[:, cols])

@@ -66,6 +66,8 @@ def tile_gnn_layer_pa_kernel(tc, BB_feature, RF_feature, W_rfrf, b_rfrf, W_bbrf,
 
         ident = const.tile([P, P], F32)
         make_identity(nc, ident[:])
+        ident_bf16 = const.tile([P, P], BF16)
+        nc.vector.tensor_copy(out=ident_bf16[:], in_=ident[:])
         sel_f32 = const.tile([P, 32], F32)
         nc.vector.tensor_reduce(
             out=sel_f32[:],
@@ -178,17 +180,32 @@ def tile_gnn_layer_pa_kernel(tc, BB_feature, RF_feature, W_rfrf, b_rfrf, W_bbrf,
 
         def mean_part(index):
             i, c = divmod(index, 2)
-            bb_v = bb_raw_tiles[i][:].rearrange("p (e c q t) -> p e c t q", e=4, c=2, t=4)
-            mean_v = mean_banks[c][:].rearrange("p (t b) -> p t b", t=4)
-            for t in range(4):
+            bb_v = bb_raw_tiles[i][:].rearrange("p (e d) -> p e d", e=4)
+            mean_v = mean_banks[c][:].rearrange("p (h b) -> p h b", h=4)
+            for h in range(4):
+                first = (4 * c + h) * P
                 for e in range(4):
                     nc.tensor.matmul(
-                        out=mean_v[:, t, 32 * i : 32 * i + 32],
-                        lhsT=bb_v[:, e, c, t, :],
+                        out=mean_v[:, h, 32 * i : 32 * i + 32],
+                        lhsT=bb_v[:, e, first : first + P],
                         rhs=sel[:],
                         start=(e == 0),
                         stop=(e == 3),
                     )
+
+        mean_columns = const.tile([P, D_BB], BF16)
+        mean_rows = const.tile([P, D_BB], BF16)
+
+        def mean_to_bf16():
+            for c in range(2):
+                nc.vector.tensor_copy(out=mean_columns[:, c * 512 : (c + 1) * 512], in_=mean_banks[c][:])
+
+        def mean_to_rows():
+            bank = tp.tile([P, D_BB], BF16, tag="tp", name="rows_bank")
+            for h in range(8):
+                cols = slice(h * P, (h + 1) * P)
+                nc.tensor.transpose(bank[:, cols], mean_columns[:, cols], ident_bf16[:])
+            nc.scalar.copy(out=mean_rows[:], in_=bank[:])
 
         transpose_and_group(rf_raw, 1, D_RF, x_grouped[0][:], 1)
 
@@ -200,6 +217,8 @@ def tile_gnn_layer_pa_kernel(tc, BB_feature, RF_feature, W_rfrf, b_rfrf, W_bbrf,
         for step in range(-2, SLOTS + 1):
             if step + 2 < SLOTS:
                 grouped[step + 2] = transpose_slot(step + 2)
+            if step == 7:
+                mean_to_rows()
             if step == -2:
                 quantise_x(0)
             if step == -1:
@@ -213,14 +232,13 @@ def tile_gnn_layer_pa_kernel(tc, BB_feature, RF_feature, W_rfrf, b_rfrf, W_bbrf,
                 codes[step + 1] = quantise_slot(step + 1, grouped[step + 1])
             if 0 <= step < SLOTS:
                 acc[step] = multiply_slot(step, codes[step][0], codes[step][1])
-            if 0 <= step < SLOTS_PER_LAYER:
+            if 0 <= step <= 6:
                 mean_part(step)
-            if step == SLOTS_PER_LAYER - 1:
-                for c in range(2):
-                    nc.vector.tensor_copy(
-                        out=x_grouped[1][:, c * 512 : (c + 1) * 512].rearrange("p (b t) -> p b t", t=4),
-                        in_=mean_banks[c][:].rearrange("p (t b) -> p b t", t=4),
-                    )
+            if step == 6:
+                mean_part(7)
+                mean_to_bf16()
+            if step == 7:
+                transpose_and_group(mean_rows, 1, D_BB, x_grouped[1][:], 1)
                 quantise_x(1)
 
         nc.scalar.activation(out=soft[:, late], in_=soft[:, late], func=ACT.Ln, bias=1.0)

@@ -13,19 +13,29 @@ P = 128
 GROUPS = 16
 D_BB = 1024
 D_RF = 2048
+DEPTH = (D_RF, D_BB)
 K_PASS = 512
-ROWS = 2
-WIDTH = P * ROWS
-SLOTS_PER_LAYER = D_RF // WIDTH
-SLOTS = 2 * SLOTS_PER_LAYER
-FIRST_BATCH = 11
-EXP_CAP = 30.0
+LN_FLOOR = 1e-30
+BANK = 512
 
+SLOTS = (
+    [(0, 256 * i, 2) for i in range(3)]
+    + [(1, 512 * i, 4) for i in range(4)]
+    + [(0, 256 * i, 2) for i in range(3, 7)]
+    + [(0, 1792, 1), (0, 1920, 1)]
+)
+EARLY = {5: range(0, 3), 8: range(3, 7)}
+LATE = range(7, 11)
+LAST = range(11, 13)
+
+COPIES = "SVSV"
+COPIES_BESIDE_LN = "VSVV"
 FLOPS = 2 * P * D_RF * (D_RF + D_BB)
 
 
 def tile_gnn_layer_pa_kernel(tc, BB_feature, RF_feature, W_rfrf, b_rfrf, W_bbrf, b_bbrf, out):
     nc = tc.nc
+    n_slots = len(SLOTS)
     with (
         tc.tile_pool(name="const", bufs=1) as const,
         tc.tile_pool(name="work", bufs=2) as work,
@@ -38,32 +48,43 @@ def tile_gnn_layer_pa_kernel(tc, BB_feature, RF_feature, W_rfrf, b_rfrf, W_bbrf,
         nc.vector.memset(bias_rows[:], 0.0)
         nc.sync.dma_start(out=bias_rows[0:16, :], in_=b_rfrf.rearrange("(r c) -> r c", c=P))
         nc.sync.dma_start(out=bias_rows[16:32, :], in_=b_bbrf.rearrange("(r c) -> r c", c=P))
-
         rf_raw = const.tile([P, D_RF], BF16)
         nc.sync.dma_start(out=rf_raw[:], in_=RF_feature)
 
-        def load_weight_slot(w, k, index):
-            w_raw = const.tile([P, ROWS * k], BF16, name="w_raw_%d_%d" % (k, index))
-            nc.sync.dma_start(
-                out=w_raw[:],
-                in_=w[index * WIDTH : (index + 1) * WIDTH, :].rearrange("(n j) k -> n (j k)", j=ROWS),
-            )
-            return w_raw
+        w_raw = {}
 
-        bb_rows = BB_feature.rearrange("b g d -> (b g) d")
-        w_raw_tiles = []
-        bb_raw_tiles = []
-        for i in range(4):
-            w_raw_tiles.append(load_weight_slot(W_rfrf, D_RF, 2 * i))
-            w_raw_tiles.append(load_weight_slot(W_rfrf, D_RF, 2 * i + 1))
-            bb_raw = const.tile([P, 4 * D_BB], BF16, name="bb_raw_%d" % i)
-            nc.sync.dma_start(
-                out=bb_raw[:],
-                in_=bb_rows[i * 512 : (i + 1) * 512, :].rearrange("(p e) d -> p (e d)", e=4),
-            )
-            bb_raw_tiles.append(bb_raw)
-        w_raw_tiles.extend([load_weight_slot(W_bbrf, D_BB, i) for i in range(SLOTS_PER_LAYER)])
+        def load_slot(s, pieces):
+            layer, first, j_rows = SLOTS[s]
+            rows = (W_rfrf, W_bbrf)[layer][first : first + P * j_rows, :].rearrange("(n j) k -> n j k", j=j_rows)
+            width = DEPTH[layer] // pieces
+            w_raw[s] = []
+            for i in range(pieces):
+                raw = const.tile([P, j_rows, width], BF16, name="w_raw_%d_%d" % (s, i))
+                nc.sync.dma_start(out=raw[:], in_=rows[:, :, i * width : (i + 1) * width])
+                w_raw[s].append(raw)
 
+        bb_raw = []
+
+        def load_bb(i):
+            raw = const.tile([P, 4 * D_BB], BF16, name="bb_raw_%d" % i)
+            rows = BB_feature.rearrange("b g d -> (b g) d")[i * 512 : (i + 1) * 512, :]
+            nc.sync.dma_start(out=raw[:], in_=rows.rearrange("(p e) d -> p (e d)", e=4))
+            bb_raw.append(raw)
+
+        load_slot(0, 2)
+        load_slot(1, 1)
+        load_slot(2, 1)
+        load_bb(0)
+        load_bb(1)
+        load_slot(3, 1)
+        load_bb(2)
+        load_bb(3)
+        for s in range(4, n_slots):
+            load_slot(s, 1)
+
+        scratch = const.tile([P, 1], F32)
+        nc.vector.memset(scratch[:], 0.0)
+        nc.scalar.activation(out=scratch[:], in_=scratch[:], func=ACT.Sigmoid)
         ident = const.tile([P, P], F32)
         make_identity(nc, ident[:])
         ident_bf16 = const.tile([P, P], BF16)
@@ -78,176 +99,260 @@ def tile_gnn_layer_pa_kernel(tc, BB_feature, RF_feature, W_rfrf, b_rfrf, W_bbrf,
         sel = const.tile([P, 32], BF16)
         nc.vector.tensor_scalar(out=sel[:], in0=sel_f32[:], scalar1=1.0 / GROUPS, scalar2=None, op0=ALU.mult)
 
-        def transpose_and_group(src, rows, k, grouped, vector_banks):
-            words = src[:].bitcast(F32)
-            grouped_words = grouped.bitcast(F32).rearrange("p (g n u) -> p g n u", n=P, u=2)
-            n_groups = rows * (k // K_PASS)
-            for pair in range(n_groups // 2):
-                bank = tp.tile([P, 512], F32, tag="tp", name="bank")
-                bank_v = bank[:].rearrange("p (h u n) -> p h u n", h=2, u=2)
-                for h in range(2):
-                    c, j = divmod(2 * pair + h, rows)
-                    for u in range(2):
-                        first = j * (k // 2) + 256 * c
-                        nc.tensor.transpose(bank_v[:, h, u, :], words[:, first + u : first + 256 : 2], ident[:])
-                copy = nc.vector.tensor_copy if pair < vector_banks else nc.scalar.copy
-                copy(
-                    out=grouped_words[:, 2 * pair : 2 * pair + 2, :, :],
-                    in_=bank[:].rearrange("p (h u n) -> p h n u", h=2, u=2),
-                )
-
-        def depth_of(slot):
-            return D_RF if slot < SLOTS_PER_LAYER else D_BB
-
-        def transpose_slot(slot):
-            k = depth_of(slot)
-            grouped = work.tile([P, ROWS * D_RF], BF16, align_bytes=64, tag="grouped", name="grouped", bufs=3)
-            if slot >= FIRST_BATCH + 3:
-                vector_banks = 4
-            elif slot < SLOTS_PER_LAYER:
-                vector_banks = 1
-            else:
-                vector_banks = slot % 2
-            transpose_and_group(w_raw_tiles[slot], ROWS, k, grouped[:, : ROWS * k], vector_banks)
-            return grouped
-
-        def quantise_slot(slot, grouped):
-            k = depth_of(slot)
-            codes = work.tile([P, ROWS * D_RF // 4], U32, align_bytes=64, tag="codes", name="codes")
-            scales = work.tile([P, ROWS * D_RF // 4], U8, align_bytes=64, tag="scales", name="scales")
-            n_words = ROWS * k // 4
-            nc.vector.quantize_mx(
-                out=codes[:, :n_words].bitcast(FP8X4), scales=scales[:, :n_words], in_=grouped[:, : ROWS * k]
-            )
-            return codes, scales
-
         z = const.tile([P, 2 * D_RF], F32)
-        soft = const.tile([P, 2 * D_RF], F32)
-        x_grouped = [const.tile([P, k], BF16, align_bytes=64, name="x_grouped_%d" % k) for k in (D_RF, D_BB)]
-        x_codes = [const.tile([P, k // 4], U32, align_bytes=64, name="x_codes_%d" % k) for k in (D_RF, D_BB)]
-        x_scales = [const.tile([P, k // 4], U8, align_bytes=64, name="x_scales_%d" % k) for k in (D_RF, D_BB)]
-        bias = const.tile([P, 2 * D_RF], F32)
-        mean_banks = [meanp.tile([P, 512], F32, tag="mean%d" % c, name="mean%d" % c) for c in range(2)]
+        q = const.tile([P, 2 * D_RF], F32)
+        bias = const.tile([P, 2 * D_RF], BF16)
+        x_grouped = [const.tile([P, k], BF16, align_bytes=64, name="x_grouped_%d" % k) for k in DEPTH]
+        x_codes = [const.tile([P, k // 4], U32, align_bytes=64, name="x_codes_%d" % k) for k in DEPTH]
+        x_scales = [const.tile([P, k // 4], U8, align_bytes=64, name="x_scales_%d" % k) for k in DEPTH]
+        mean_banks = [meanp.tile([P, BANK], F32, tag="mean%d" % c, name="mean%d" % c) for c in range(2)]
+        mean_columns = const.tile([P, D_BB], BF16)
+        mean_rows = const.tile([P, D_BB], BF16)
+
+        banks_used = []
+
+        def next_bank():
+            turn = len(banks_used)
+            banks_used.append(turn)
+            if "mean_done" in progress and turn % 6 >= 4:
+                return meanp.tile([P, BANK], F32, tag="mean%d" % (turn % 6 - 4), name="late_bank")
+            return tp.tile([P, BANK], F32, tag="tp", name="bank")
+
+        progress = set()
+
+        def copy_on(engine):
+            return nc.vector.tensor_copy if engine == "V" else nc.scalar.copy
+
+        def transpose_bank(words_of, j_rows, index, grouped, engine):
+            bank = next_bank()
+            for h in range(2):
+                c, j = divmod(2 * index + h, j_rows)
+                for u in range(2):
+                    columns = slice((2 * h + u) * P, (2 * h + u + 1) * P)
+                    nc.tensor.transpose(bank[:, columns], words_of(c, j, u), ident[:])
+            words = grouped.bitcast(F32).rearrange("p (g n u) -> p g n u", n=P, u=2)
+            copy_on(engine)(
+                out=words[:, 2 * index : 2 * index + 2, :, :],
+                in_=bank[:].rearrange("p (h u n) -> p h n u", h=2, u=2),
+            )
+
+        def words_of_rows(tile):
+            words = tile[:].bitcast(F32)
+            return lambda c, j, u: words[:, 256 * c + u : 256 * c + 256 : 2]
+
+        def words_of_slot(s):
+            layer = SLOTS[s][0]
+            passes = DEPTH[layer] // K_PASS // len(w_raw[s])
+
+            def words_of(c, j, u):
+                words = w_raw[s][c // passes][:, j, :].bitcast(F32)
+                c_in = c % passes
+                return words[:, 256 * c_in + u : 256 * c_in + 256 : 2]
+
+            return words_of
+
+        def columns_of(s):
+            layer, first, j_rows = SLOTS[s]
+            return slice(layer * D_RF + first, layer * D_RF + first + P * j_rows)
 
         def quantise_x(layer):
             nc.vector.quantize_mx(
                 out=x_codes[layer][:].bitcast(FP8X4), scales=x_scales[layer][:], in_=x_grouped[layer][:]
             )
 
-        def spread_biases():
-            rows_f32 = const.tile([P, P], F32)
-            nc.vector.tensor_copy(out=rows_f32[:], in_=bias_rows[:])
-            columns_bank = tp.tile([P, 512], F32, tag="tp", name="columns_bank")
-            nc.tensor.transpose(columns_bank[:, :P], rows_f32[:], ident[:])
-            columns = const.tile([P, 32], F32)
-            nc.vector.tensor_copy(out=columns[:], in_=columns_bank[:, :32])
-            for index in range(8):
-                bank = tp.tile([P, 512], F32, tag="tp", name="bias_bank")
-                for quarter in range(4):
-                    r = 4 * index + quarter
-                    nc.tensor.transpose(
-                        bank[:, quarter * P : (quarter + 1) * P], columns[:, r : r + 1].to_broadcast([P, P]), ident[:]
-                    )
-                copy = nc.vector.tensor_copy if index % 2 == 0 else nc.scalar.copy
-                copy(out=bias[:, index * 512 : (index + 1) * 512], in_=bank[:])
+        def quantise_slot(s):
+            layer, first, j_rows = SLOTS[s]
+            n_words = j_rows * DEPTH[layer] // 4
+            codes = work.tile([P, 1024], U32, align_bytes=64, tag="codes", name="codes")
+            scales = work.tile([P, 1024], U8, align_bytes=64, tag="scales", name="scales")
+            nc.vector.quantize_mx(
+                out=codes[:, :n_words].bitcast(FP8X4), scales=scales[:, :n_words], in_=grouped[s][:, : 4 * n_words]
+            )
+            return codes, scales
 
-        def multiply_slot(slot, w_codes, w_scales):
-            layer = slot // SLOTS_PER_LAYER
-            passes = depth_of(slot) // K_PASS
-            acc = accp.tile([P, WIDTH], F32, tag="acc", name="acc")
+        def multiply_slot(s):
+            layer, first, j_rows = SLOTS[s]
+            width = P * j_rows
+            passes = DEPTH[layer] // K_PASS
+            w_codes, w_scales = codes[s]
+            result = accp.tile([P, BANK], F32, tag="acc", name="acc")
             for c in range(passes):
                 nc.tensor.matmul_mx(
-                    out=acc[:],
+                    out=result[:, :width],
                     lhsT=x_codes[layer][:, c * P : (c + 1) * P].bitcast(FP8X4),
                     lhsT_scale=x_scales[layer][:, c * P : (c + 1) * P],
-                    rhs=w_codes[:, c * WIDTH : (c + 1) * WIDTH].bitcast(FP8X4),
-                    rhs_scale=w_scales[:, c * WIDTH : (c + 1) * WIDTH],
+                    rhs=w_codes[:, c * width : (c + 1) * width].bitcast(FP8X4),
+                    rhs_scale=w_scales[:, c * width : (c + 1) * width],
                     start=(c == 0),
                     stop=(c == passes - 1),
                 )
-            return acc
+            return result
 
-        def add_bias_and_exp(slot, acc):
-            cols = slice(slot * WIDTH, (slot + 1) * WIDTH)
+        def add_bias(s):
+            j_rows = SLOTS[s][2]
+            columns = columns_of(s)
             nc.vector.tensor_tensor(
-                out=z[:, cols].rearrange("p (n j) -> p n j", j=ROWS),
-                in0=acc[:].rearrange("p (j n) -> p n j", j=ROWS),
-                in1=bias[:, cols].rearrange("p (n j) -> p n j", j=ROWS),
+                out=z[:, columns].rearrange("p (n j) -> p n j", j=j_rows),
+                in0=acc[s][:, : P * j_rows].rearrange("p (j n) -> p n j", j=j_rows),
+                in1=bias[:, columns].rearrange("p (n j) -> p n j", j=j_rows),
                 op=ALU.add,
             )
-            nc.vector.tensor_scalar(out=soft[:, cols], in0=z[:, cols], scalar1=EXP_CAP, scalar2=None, op0=ALU.min)
-            nc.scalar.activation(out=soft[:, cols], in_=soft[:, cols], func=ACT.Exp)
 
-        def mean_part(index):
-            i, c = divmod(index, 2)
-            bb_v = bb_raw_tiles[i][:].rearrange("p (e d) -> p e d", e=4)
-            mean_v = mean_banks[c][:].rearrange("p (h b) -> p h b", h=4)
-            for h in range(4):
-                first = (4 * c + h) * P
+        def sigmoid(s):
+            columns = columns_of(s)
+            nc.scalar.activation(out=q[:, columns], in_=z[:, columns], func=ACT.Sigmoid, scale=-1.0)
+            if s in LAST:
+                nc.scalar.activation(out=q[:, columns], in_=q[:, columns], func=ACT.Square)
+
+        def ln(columns):
+            nc.scalar.activation(out=q[:, columns], in_=q[:, columns], func=ACT.Ln, bias=LN_FLOOR)
+
+        def tanh(columns):
+            nc.scalar.activation(out=q[:, columns], in_=q[:, columns], func=ACT.Tanh, scale=-1.0)
+
+        def times_z(columns):
+            nc.vector.tensor_tensor(out=q[:, columns], in0=z[:, columns], in1=q[:, columns], op=ALU.mult)
+
+        def finish_by_reciprocal(s):
+            columns = columns_of(s)
+            part = q[:, columns]
+            nc.vector.tensor_scalar(out=part, in0=part, scalar1=0.5, scalar2=0.5, op0=ALU.mult, op1=ALU.add)
+            nc.vector.reciprocal(out=part, in_=part)
+            nc.vector.scalar_tensor_tensor(
+                out=part, in0=part, scalar=-1.0, in1=z[:, columns], op0=ALU.add, op1=ALU.mult
+            )
+
+        def add_and_store(first, last):
+            nc.vector.tensor_tensor(
+                out=z[:, first:last], in0=q[:, first:last], in1=q[:, D_RF + first : D_RF + last], op=ALU.add
+            )
+            nc.sync.dma_start(out=out[:, first:last], in_=z[:, first:last])
+
+        def column_runs(slots, longest):
+            runs = []
+            for s in slots:
+                columns = columns_of(s)
+                if runs and runs[-1].stop == columns.start and columns.stop - runs[-1].start <= longest:
+                    runs[-1] = slice(runs[-1].start, columns.stop)
+                else:
+                    runs.append(columns)
+            return runs
+
+        bias_columns = const.tile([P, 32], BF16)
+
+        def turn_biases():
+            bank = tp.tile([P, P], BF16, tag="tp", name="bias_turn")
+            nc.tensor.transpose(bank[:], bias_rows[:], ident_bf16[:])
+            nc.vector.tensor_copy(out=bias_columns[:], in_=bank[:, :32])
+
+        def spread_biases(index, engine):
+            bank = tp.tile([P, 1024], BF16, tag="tp", name="bias_bank")
+            for i in range(8):
+                r = 8 * index + i
+                nc.tensor.transpose(
+                    bank[:, i * P : (i + 1) * P], bias_columns[:, r : r + 1].to_broadcast([P, P]), ident_bf16[:]
+                )
+            copy_on(engine)(out=bias[:, index * 1024 : (index + 1) * 1024], in_=bank[:])
+
+        mean_queue = []
+
+        def mean_part(n):
+            for unused in range(min(n, len(mean_queue))):
+                i, h = mean_queue.pop(0)
+                rows = bb_raw[i][:].rearrange("p (e d) -> p e d", e=4)
+                place = (h % 4) * P + 32 * i
                 for e in range(4):
                     nc.tensor.matmul(
-                        out=mean_v[:, h, 32 * i : 32 * i + 32],
-                        lhsT=bb_v[:, e, first : first + P],
+                        out=mean_banks[h // 4][:, place : place + 32],
+                        lhsT=rows[:, e, h * P : (h + 1) * P],
                         rhs=sel[:],
                         start=(e == 0),
                         stop=(e == 3),
                     )
 
-        mean_columns = const.tile([P, D_BB], BF16)
-        mean_rows = const.tile([P, D_BB], BF16)
-
-        def mean_to_bf16():
-            for c in range(2):
-                nc.vector.tensor_copy(out=mean_columns[:, c * 512 : (c + 1) * 512], in_=mean_banks[c][:])
-
-        def mean_to_rows():
-            bank = tp.tile([P, D_BB], BF16, tag="tp", name="rows_bank")
-            for h in range(8):
-                cols = slice(h * P, (h + 1) * P)
-                nc.tensor.transpose(bank[:, cols], mean_columns[:, cols], ident_bf16[:])
-            nc.scalar.copy(out=mean_rows[:], in_=bank[:])
-
-        transpose_and_group(rf_raw, 1, D_RF, x_grouped[0][:], 1)
-
-        early = slice(0, FIRST_BATCH * WIDTH)
-        late = slice(FIRST_BATCH * WIDTH, SLOTS * WIDTH)
         grouped = {}
         codes = {}
         acc = {}
-        for step in range(-2, SLOTS + 1):
-            if step + 2 < SLOTS:
-                grouped[step + 2] = transpose_slot(step + 2)
-            if step == 7:
-                mean_to_rows()
+        scalar_queue = []
+        vector_queue = []
+        held = []
+
+        turn_biases()
+        transpose_bank(words_of_rows(rf_raw), 1, 0, x_grouped[0][:], "V")
+        transpose_bank(words_of_rows(rf_raw), 1, 1, x_grouped[0][:], "S")
+        for step in range(-2, n_slots + 2):
+            t = step + 2
+            n_banks = 0
+            if t < n_slots:
+                layer, first, j_rows = SLOTS[t]
+                n_banks = j_rows * DEPTH[layer] // 1024
+                grouped[t] = work.tile([P, 4096], BF16, align_bytes=64, tag="grouped", name="grouped", bufs=3)
+            if step == 0:
+                mean_queue.extend([(i, h) for i in range(2) for h in range(8)])
+            if step == 1:
+                mean_queue.extend([(i, h) for i in range(2, 4) for h in range(8)])
             if step == -2:
                 quantise_x(0)
-            if step == -1:
-                spread_biases()
-            if step >= 1:
-                add_bias_and_exp(step - 1, acc[step - 1])
-            if step == FIRST_BATCH:
-                nc.scalar.activation(out=soft[:, early], in_=soft[:, early], func=ACT.Ln, bias=1.0)
-                nc.scalar.activation(out=soft[:, early], in_=soft[:, early], func=ACT.Tanh)
-            if 0 <= step + 1 < SLOTS:
-                codes[step + 1] = quantise_slot(step + 1, grouped[step + 1])
-            if 0 <= step < SLOTS:
-                acc[step] = multiply_slot(step, codes[step][0], codes[step][1])
-            if 0 <= step <= 6:
-                mean_part(step)
-            if step == 6:
-                mean_part(7)
-                mean_to_bf16()
-            if step == 7:
-                transpose_and_group(mean_rows, 1, D_BB, x_grouped[1][:], 1)
+            if 0 <= step - 1 < n_slots:
+                add_bias(step - 1)
+            if step == 2:
+                rows_bank = tp.tile([P, D_BB], BF16, tag="tp", name="rows_bank")
+                for h in range(8):
+                    columns = slice(h * P, (h + 1) * P)
+                    nc.tensor.transpose(rows_bank[:, columns], mean_columns[:, columns], ident_bf16[:])
+                nc.scalar.copy(out=mean_rows[:], in_=rows_bank[:])
+            engines = COPIES_BESIDE_LN if scalar_queue or step in EARLY else COPIES
+            for index in range(4):
+                if index < n_banks:
+                    transpose_bank(words_of_slot(t), j_rows, index, grouped[t][:, : 1024 * n_banks], engines[index])
+                    mean_part(4)
+                if index == 0 and vector_queue:
+                    work_item, run = vector_queue.pop(0)
+                    work_item(run)
+                if index == 0 and 0 <= step - 2 < n_slots:
+                    if scalar_queue and scalar_queue[0][0] is ln:
+                        held.append(step - 2)
+                    else:
+                        sigmoid(step - 2)
+                if index == 0 and step in EARLY:
+                    runs = column_runs(EARLY[step], 512)
+                    scalar_queue.extend([(ln, run) for run in runs] + [(tanh, run) for run in runs])
+                if index in (0, 2) and scalar_queue:
+                    work_item, run = scalar_queue.pop(0)
+                    work_item(run)
+                    if work_item is tanh:
+                        vector_queue.append((times_z, run))
+                    elif scalar_queue[0][0] is tanh:
+                        for s in held:
+                            sigmoid(s)
+                        held.clear()
+                if index == 1 and 0 <= step + 1 < n_slots:
+                    codes[step + 1] = quantise_slot(step + 1)
+            mean_part(len(mean_queue))
+            if step in (-2, -1):
+                spread_biases(2 * step + 4, "V")
+                spread_biases(2 * step + 5, "S")
+            if 0 <= step < n_slots:
+                acc[step] = multiply_slot(step)
+            if step == 1:
+                nc.vector.tensor_copy(out=mean_columns[:, :BANK], in_=mean_banks[0][:])
+                nc.scalar.copy(out=mean_columns[:, BANK:], in_=mean_banks[1][:])
+            if step == 2:
+                progress.add("mean_done")
+                transpose_bank(words_of_rows(mean_rows), 1, 0, x_grouped[1][:], "V")
                 quantise_x(1)
 
-        nc.scalar.activation(out=soft[:, late], in_=soft[:, late], func=ACT.Ln, bias=1.0)
-        nc.vector.tensor_tensor(out=soft[:, early], in0=z[:, early], in1=soft[:, early], op=ALU.mult)
-        for slot in range(SLOTS_PER_LAYER, SLOTS):
-            cols = slice(slot * WIDTH, (slot + 1) * WIDTH)
-            out_cols = slice((slot - SLOTS_PER_LAYER) * WIDTH, (slot - SLOTS_PER_LAYER + 1) * WIDTH)
-            if slot >= FIRST_BATCH:
-                nc.scalar.activation(out=soft[:, cols], in_=soft[:, cols], func=ACT.Tanh)
-                nc.vector.tensor_tensor(out=soft[:, cols], in0=z[:, cols], in1=soft[:, cols], op=ALU.mult)
-            nc.vector.tensor_tensor(out=soft[:, cols], in0=soft[:, cols], in1=soft[:, out_cols], op=ALU.add)
-            nc.sync.dma_start(out=out[:, out_cols], in_=soft[:, cols])
+        late_runs = column_runs(LATE, 512)
+        for run in late_runs:
+            ln(run)
+        for run in late_runs:
+            tanh(run)
+        for s in LAST:
+            finish_by_reciprocal(s)
+        for work_item, run in vector_queue:
+            work_item(run)
+        add_and_store(0, 768)
+        add_and_store(1792, 2048)
+        for run in late_runs:
+            times_z(run)
+            add_and_store(run.start, run.stop)

@@ -305,7 +305,6 @@ def tile_gnn_layer_pa_kernel(tc, BB_feature, RF_feature, W_rfrf, b_rfrf, W_bbrf,
             for index in range(4):
                 if index < n_banks:
                     transpose_bank(words_of_slot(t), j_rows, index, grouped[t][:, : 1024 * n_banks], engines[index])
-                    mean_part(4)
                 if index == 0 and vector_queue:
                     work_item, run = vector_queue.pop(0)
                     work_item(run)

@@ -18,17 +18,17 @@ K_PASS = 512
 LN_FLOOR = 1e-30
 BANK = 512
 
+N_FIRST = 7
 SLOTS = (
-    [(0, 256 * i, 2) for i in range(3)]
+    [(0, 256 * i, 2) for i in range(N_FIRST)]
     + [(1, 512 * i, 4) for i in range(4)]
-    + [(0, 256 * i, 2) for i in range(3, 7)]
     + [(0, 1792, 1), (0, 1920, 1)]
 )
-EARLY = {5: range(0, 3), 8: range(3, 7)}
+EARLY = {4: range(0, 3), 8: range(3, 7)}
 LATE = range(7, 11)
 LAST = range(11, 13)
 
-COPIES = "SVSV"
+COPIES = "SSSV"
 COPIES_BESIDE_LN = "VSVV"
 FLOPS = 2 * P * D_RF * (D_RF + D_BB)
 
@@ -44,12 +44,15 @@ def tile_gnn_layer_pa_kernel(tc, BB_feature, RF_feature, W_rfrf, b_rfrf, W_bbrf,
         tc.psum_pool(name="meanp", bufs=1) as meanp,
         tc.manual_schedule(),
     ):
+        rf_raw = []
+        for half in range(2):
+            raw = const.tile([P, D_RF // 2], BF16, name="rf_raw_%d" % half)
+            nc.sync.dma_start(out=raw[:], in_=RF_feature[:, half * D_RF // 2 : (half + 1) * D_RF // 2])
+            rf_raw.append(raw)
         bias_rows = const.tile([P, P], BF16)
         nc.vector.memset(bias_rows[:], 0.0)
         nc.sync.dma_start(out=bias_rows[0:16, :], in_=b_rfrf.rearrange("(r c) -> r c", c=P))
         nc.sync.dma_start(out=bias_rows[16:32, :], in_=b_bbrf.rearrange("(r c) -> r c", c=P))
-        rf_raw = const.tile([P, D_RF], BF16)
-        nc.sync.dma_start(out=rf_raw[:], in_=RF_feature)
 
         w_raw = {}
 
@@ -72,15 +75,11 @@ def tile_gnn_layer_pa_kernel(tc, BB_feature, RF_feature, W_rfrf, b_rfrf, W_bbrf,
             bb_raw.append(raw)
 
         load_slot(0, 2)
-        load_slot(1, 1)
-        load_slot(2, 1)
-        load_bb(0)
-        load_bb(1)
-        load_slot(3, 1)
-        load_bb(2)
-        load_bb(3)
-        for s in range(4, n_slots):
+        for s in range(1, n_slots):
             load_slot(s, 1)
+            if s in (N_FIRST - 1, N_FIRST):
+                load_bb(2 * (s - N_FIRST + 1))
+                load_bb(2 * (s - N_FIRST + 1) + 1)
 
         scratch = const.tile([P, 1], F32)
         nc.vector.memset(scratch[:], 0.0)
@@ -277,9 +276,12 @@ def tile_gnn_layer_pa_kernel(tc, BB_feature, RF_feature, W_rfrf, b_rfrf, W_bbrf,
         vector_queue = []
         held = []
 
+        for half in range(2):
+            words_of = words_of_rows(rf_raw[half])
+            transpose_bank(lambda c, j, u: words_of(c % 2, j, u), 1, half, x_grouped[0][:], "VS"[half])
         turn_biases()
-        transpose_bank(words_of_rows(rf_raw), 1, 0, x_grouped[0][:], "V")
-        transpose_bank(words_of_rows(rf_raw), 1, 1, x_grouped[0][:], "S")
+        for index in range(4):
+            spread_biases(index, "VS"[index % 2])
         for step in range(-2, n_slots + 2):
             t = step + 2
             n_banks = 0
@@ -287,15 +289,15 @@ def tile_gnn_layer_pa_kernel(tc, BB_feature, RF_feature, W_rfrf, b_rfrf, W_bbrf,
                 layer, first, j_rows = SLOTS[t]
                 n_banks = j_rows * DEPTH[layer] // 1024
                 grouped[t] = work.tile([P, 4096], BF16, align_bytes=64, tag="grouped", name="grouped", bufs=3)
-            if step == 0:
+            if step == N_FIRST - 3:
                 mean_queue.extend([(i, h) for i in range(2) for h in range(8)])
-            if step == 1:
+            if step == N_FIRST - 2:
                 mean_queue.extend([(i, h) for i in range(2, 4) for h in range(8)])
             if step == -2:
                 quantise_x(0)
             if 0 <= step - 1 < n_slots:
                 add_bias(step - 1)
-            if step == 2:
+            if step == N_FIRST - 1:
                 rows_bank = tp.tile([P, D_BB], BF16, tag="tp", name="rows_bank")
                 for h in range(8):
                     columns = slice(h * P, (h + 1) * P)
@@ -328,15 +330,12 @@ def tile_gnn_layer_pa_kernel(tc, BB_feature, RF_feature, W_rfrf, b_rfrf, W_bbrf,
                 if index == 1 and 0 <= step + 1 < n_slots:
                     codes[step + 1] = quantise_slot(step + 1)
             mean_part(len(mean_queue))
-            if step in (-2, -1):
-                spread_biases(2 * step + 4, "V")
-                spread_biases(2 * step + 5, "S")
             if 0 <= step < n_slots:
                 acc[step] = multiply_slot(step)
-            if step == 1:
+            if step == N_FIRST - 2:
                 nc.vector.tensor_copy(out=mean_columns[:, :BANK], in_=mean_banks[0][:])
                 nc.scalar.copy(out=mean_columns[:, BANK:], in_=mean_banks[1][:])
-            if step == 2:
+            if step == N_FIRST - 1:
                 progress.add("mean_done")
                 transpose_bank(words_of_rows(mean_rows), 1, 0, x_grouped[1][:], "V")
                 quantise_x(1)
@@ -350,8 +349,8 @@ def tile_gnn_layer_pa_kernel(tc, BB_feature, RF_feature, W_rfrf, b_rfrf, W_bbrf,
             finish_by_reciprocal(s)
         for work_item, run in vector_queue:
             work_item(run)
-        add_and_store(0, 768)
-        add_and_store(1792, 2048)
-        for run in late_runs:
-            times_z(run)
-            add_and_store(run.start, run.stop)
+        for i in range(len(late_runs) + 1):
+            if i < len(late_runs):
+                times_z(late_runs[i])
+            if i > 0:
+                add_and_store(late_runs[i - 1].start - D_RF, late_runs[i - 1].stop - D_RF)

@@ -18,18 +18,39 @@ K_PASS = 512
 LN_FLOOR = 1e-30
 BANK = 512
 
-N_FIRST = 7
-SLOTS = (
-    [(0, 256 * i, 2) for i in range(N_FIRST)]
-    + [(1, 512 * i, 4) for i in range(4)]
-    + [(0, 1792, 1), (0, 1920, 1)]
-)
-EARLY = {4: range(0, 3), 8: range(3, 7)}
-LATE = range(7, 11)
-LAST = range(11, 13)
+N_FIRST = 2
+LAYER0 = [(0, 256 * i, 2) for i in range(7)] + [(0, 1792, 1), (0, 1920, 1)]
+SLOTS = LAYER0[:N_FIRST] + [(1, 512 * i, 4) for i in range(4)] + LAYER0[N_FIRST:]
+EARLY = {8: range(0, 7)}
+LATE = range(7, 13)
+COPIES_LATE = "VVVV"
+LATEFROM = 9
+PROD = "V"
+GCH = 256
+SQ1 = "S"
+SQ1LAST = "S"
+LAGN = 1
+ORD = "VV.."
+ORDFROM = 4
+ORDTO = 7
+POSTSQ = 1
+SUMB = 1
+SQ = "S"
+DRAIN = 0
+LAGB = 0
+SIGD = 0
+SIGI = 2
+MXFIRST = 0
+SP = (0,1,2,3)
+CHL = 256
+SQ2 = "S"
+ARS_EARLY = ()
+VSTOP = 9
+BBE = 0
+MB = 0
 
-COPIES = "SSSV"
-COPIES_BESIDE_LN = "VSVV"
+COPIES = "SSSS"
+COPIES_BESIDE_LN = "SSSS"
 FLOPS = 2 * P * D_RF * (D_RF + D_BB)
 
 
@@ -44,13 +65,8 @@ def tile_gnn_layer_pa_kernel(tc, BB_feature, RF_feature, W_rfrf, b_rfrf, W_bbrf,
         tc.psum_pool(name="meanp", bufs=1) as meanp,
         tc.manual_schedule(),
     ):
-        rf_raw = []
-        for half in range(2):
-            raw = const.tile([P, D_RF // 2], BF16, name="rf_raw_%d" % half)
-            nc.sync.dma_start(out=raw[:], in_=RF_feature[:, half * D_RF // 2 : (half + 1) * D_RF // 2])
-            rf_raw.append(raw)
         bias_rows = const.tile([P, P], BF16)
-        nc.vector.memset(bias_rows[:], 0.0)
+        nc.gpsimd.memset(bias_rows[:], 0.0)
         nc.sync.dma_start(out=bias_rows[0:16, :], in_=b_rfrf.rearrange("(r c) -> r c", c=P))
         nc.sync.dma_start(out=bias_rows[16:32, :], in_=b_bbrf.rearrange("(r c) -> r c", c=P))
 
@@ -75,11 +91,19 @@ def tile_gnn_layer_pa_kernel(tc, BB_feature, RF_feature, W_rfrf, b_rfrf, W_bbrf,
             bb_raw.append(raw)
 
         load_slot(0, 2)
+        rf_raw = []
+        for half in range(2):
+            raw = const.tile([P, D_RF // 2], BF16, name="rf_raw_%d" % half)
+            nc.sync.dma_start(out=raw[:], in_=RF_feature[:, half * D_RF // 2 : (half + 1) * D_RF // 2])
+            rf_raw.append(raw)
         for s in range(1, n_slots):
             load_slot(s, 1)
-            if s in (N_FIRST - 1, N_FIRST):
-                load_bb(2 * (s - N_FIRST + 1))
-                load_bb(2 * (s - N_FIRST + 1) + 1)
+            if s == N_FIRST - 1 - BBE:
+                load_bb(0)
+                load_bb(1)
+            if s == N_FIRST - BBE:
+                load_bb(2)
+                load_bb(3)
 
         scratch = const.tile([P, 1], F32)
         nc.vector.memset(scratch[:], 0.0)
@@ -120,7 +144,7 @@ def tile_gnn_layer_pa_kernel(tc, BB_feature, RF_feature, W_rfrf, b_rfrf, W_bbrf,
         progress = set()
 
         def copy_on(engine):
-            return nc.vector.tensor_copy if engine == "V" else nc.scalar.copy
+            return {"V": nc.vector.tensor_copy, "S": nc.scalar.copy, "G": nc.gpsimd.tensor_copy}[engine]
 
         def transpose_bank(words_of, j_rows, index, grouped, engine):
             bank = next_bank()
@@ -139,11 +163,33 @@ def tile_gnn_layer_pa_kernel(tc, BB_feature, RF_feature, W_rfrf, b_rfrf, W_bbrf,
             words = tile[:].bitcast(F32)
             return lambda c, j, u: words[:, 256 * c + u : 256 * c + 256 : 2]
 
+        ordered = {}
+
+        def order_words(s, index, engine):
+            j_rows = SLOTS[s][2]
+            if s not in ordered:
+                ordered[s] = [work.tile([P, 4, BANK], F32, tag="ordered", name="ordered"), set()]
+            passes = DEPTH[SLOTS[s][0]] // K_PASS // len(w_raw[s])
+            words_raw = lambda c: w_raw[s][c // passes][:].rearrange("p j k -> p (j k)").bitcast(F32).rearrange("p (j c w u) -> p c j u w", j=j_rows, c=passes, u=2)[:, c % passes, :, :, :]
+            ordered[s][1].add(index)
+            c, j = divmod(2 * index, j_rows)
+            if j_rows == 1:
+                words = w_raw[s][0][:].rearrange("p j k -> p (j k)").bitcast(F32).rearrange("p (c w u) -> p c u w", c=passes, u=2)[:, c : c + 2, :, :]
+            else:
+                words = words_raw(c)[:, j : j + 2, :, :]
+            copy_on(engine)(
+                out=ordered[s][0][:, index, :].rearrange("p (h u w) -> p h u w", h=2, u=2),
+                in_=words,
+            )
+
         def words_of_slot(s):
             layer = SLOTS[s][0]
             passes = DEPTH[layer] // K_PASS // len(w_raw[s])
 
             def words_of(c, j, u):
+                index, h = divmod(c * SLOTS[s][2] + j, 2)
+                if s in ordered and index in ordered[s][1]:
+                    return ordered[s][0][:, index, (2 * h + u) * P : (2 * h + u + 1) * P]
                 words = w_raw[s][c // passes][:, j, :].bitcast(F32)
                 c_in = c % passes
                 return words[:, 256 * c_in + u : 256 * c_in + 256 : 2]
@@ -200,8 +246,16 @@ def tile_gnn_layer_pa_kernel(tc, BB_feature, RF_feature, W_rfrf, b_rfrf, W_bbrf,
         def sigmoid(s):
             columns = columns_of(s)
             nc.scalar.activation(out=q[:, columns], in_=z[:, columns], func=ACT.Sigmoid, scale=-1.0)
-            if s in LAST:
-                nc.scalar.activation(out=q[:, columns], in_=q[:, columns], func=ACT.Square)
+            if s in LATE or s in ARS_EARLY:
+                sq = SQ1LAST if s >= 10 else SQ1
+                if sq == "S":
+                    nc.scalar.activation(out=q[:, columns], in_=q[:, columns], func=ACT.Square)
+                elif sq == "V":
+                    nc.vector.tensor_tensor(out=q[:, columns], in0=q[:, columns], in1=q[:, columns], op=ALU.mult)
+                else:
+                    nc.gpsimd.tensor_tensor(out=q[:, columns], in0=q[:, columns], in1=q[:, columns], op=ALU.mult)
+                if SQ2 == "S" and not POSTSQ:
+                    nc.scalar.activation(out=q[:, columns], in_=q[:, columns], func=ACT.Square, bias=1.0)
 
         def ln(columns):
             nc.scalar.activation(out=q[:, columns], in_=q[:, columns], func=ACT.Ln, bias=LN_FLOOR)
@@ -210,13 +264,26 @@ def tile_gnn_layer_pa_kernel(tc, BB_feature, RF_feature, W_rfrf, b_rfrf, W_bbrf,
             nc.scalar.activation(out=q[:, columns], in_=q[:, columns], func=ACT.Tanh, scale=-1.0)
 
         def times_z(columns):
-            nc.vector.tensor_tensor(out=q[:, columns], in0=z[:, columns], in1=q[:, columns], op=ALU.mult)
+            if PROD == "V":
+                nc.vector.tensor_tensor(out=q[:, columns], in0=z[:, columns], in1=q[:, columns], op=ALU.mult)
+            else:
+                for a in range(columns.start, columns.stop, GCH):
+                    part = slice(a, min(a + GCH, columns.stop))
+                    nc.gpsimd.tensor_tensor(out=q[:, part], in0=z[:, part], in1=q[:, part], op=ALU.mult)
 
-        def finish_by_reciprocal(s):
-            columns = columns_of(s)
+        def rsqrt(columns):
+            nc.scalar.activation(
+                out=q[:, columns], in_=q[:, columns], func=ACT.Abs_reciprocal_sqrt, scale=0.5 if POSTSQ else 0.25, bias=0.5 if POSTSQ else 0.0
+            )
+
+        def squared(columns, engine):
+            if engine == "S":
+                nc.scalar.activation(out=q[:, columns], in_=q[:, columns], func=ACT.Square)
+            else:
+                nc.vector.tensor_tensor(out=q[:, columns], in0=q[:, columns], in1=q[:, columns], op=ALU.mult)
+
+        def less_one_times_z(columns):
             part = q[:, columns]
-            nc.vector.tensor_scalar(out=part, in0=part, scalar1=0.5, scalar2=0.5, op0=ALU.mult, op1=ALU.add)
-            nc.vector.reciprocal(out=part, in_=part)
             nc.vector.scalar_tensor_tensor(
                 out=part, in0=part, scalar=-1.0, in1=z[:, columns], op0=ALU.add, op1=ALU.mult
             )
@@ -276,12 +343,48 @@ def tile_gnn_layer_pa_kernel(tc, BB_feature, RF_feature, W_rfrf, b_rfrf, W_bbrf,
         vector_queue = []
         held = []
 
-        for half in range(2):
-            words_of = words_of_rows(rf_raw[half])
-            transpose_bank(lambda c, j, u: words_of(c % 2, j, u), 1, half, x_grouped[0][:], "VS"[half])
+        finished = set()
+        ready = []
+
+        def product(work_item, run):
+            work_item(run)
+            for a in range(run.start, run.stop, P):
+                finished.add(a)
+                if (a + D_RF) % (2 * D_RF) in finished:
+                    ready.append(a % D_RF)
+
+        def sums(keep):
+            blocks = sorted(ready[: len(ready) - keep])
+            rest = ready[len(ready) - keep :]
+            ready.clear()
+            ready.extend(rest)
+            while blocks:
+                n = 1
+                while n < len(blocks) and n < 6 and blocks[n] == blocks[0] + n * P:
+                    n += 1
+                add_and_store(blocks[0], blocks[0] + n * P)
+                blocks = blocks[n:]
+
+        def run_scalar():
+            work_item, run = scalar_queue.pop(0)
+            work_item(run)
+            if work_item is tanh:
+                vector_queue.append((times_z, run))
+            elif work_item is rsqrt:
+                vector_queue.append((less_one_times_z, run))
+            if not scalar_queue or (work_item is ln and scalar_queue[0][0] is tanh):
+                for s in held:
+                    sigmoid(s)
+                held.clear()
+
         turn_biases()
         for index in range(4):
             spread_biases(index, "VS"[index % 2])
+        def lag(s):
+            if DRAIN and s == N_FIRST - 1:
+                return 2
+            return LAGN if s < N_FIRST else LAGB
+
         for step in range(-2, n_slots + 2):
             t = step + 2
             n_banks = 0
@@ -293,10 +396,11 @@ def tile_gnn_layer_pa_kernel(tc, BB_feature, RF_feature, W_rfrf, b_rfrf, W_bbrf,
                 mean_queue.extend([(i, h) for i in range(2) for h in range(8)])
             if step == N_FIRST - 2:
                 mean_queue.extend([(i, h) for i in range(2, 4) for h in range(8)])
-            if step == -2:
+            if step == -1:
                 quantise_x(0)
-            if 0 <= step - 1 < n_slots:
-                add_bias(step - 1)
+            for s in range(n_slots):
+                if s + 1 - lag(s) == step:
+                    add_bias(s)
             if step == N_FIRST - 1:
                 rows_bank = tp.tile([P, D_BB], BF16, tag="tp", name="rows_bank")
                 for h in range(8):
@@ -304,34 +408,50 @@ def tile_gnn_layer_pa_kernel(tc, BB_feature, RF_feature, W_rfrf, b_rfrf, W_bbrf,
                     nc.tensor.transpose(rows_bank[:, columns], mean_columns[:, columns], ident_bf16[:])
                 nc.scalar.copy(out=mean_rows[:], in_=rows_bank[:])
             engines = COPIES_BESIDE_LN if scalar_queue or step in EARLY else COPIES
+            if t >= LATEFROM:
+                engines = COPIES_LATE
             for index in range(4):
+                if ORDFROM <= t + 1 < min(n_slots, ORDTO) and index < SLOTS[t + 1][2] * DEPTH[SLOTS[t + 1][0]] // 1024 and ORD[index] != ".":
+                    order_words(t + 1, index, ORD[index])
                 if index < n_banks:
                     transpose_bank(words_of_slot(t), j_rows, index, grouped[t][:, : 1024 * n_banks], engines[index])
-                if index == 0 and vector_queue:
+                if index:
+                    mean_part(MB)
+                if index == 0 and vector_queue and step < VSTOP:
                     work_item, run = vector_queue.pop(0)
-                    work_item(run)
-                if index == 0 and 0 <= step - 2 < n_slots:
-                    if scalar_queue and scalar_queue[0][0] is ln:
-                        held.append(step - 2)
-                    else:
-                        sigmoid(step - 2)
+                    product(work_item, run)
+                if index == 2 and SUMB and step < VSTOP:
+                    sums(0)
+                for s in range(n_slots):
+                    if index == SIGI and s + 1 + SIGD - lag(s) == step:
+                        if scalar_queue and scalar_queue[0][0] is not tanh:
+                            held.append(s)
+                        else:
+                            sigmoid(s)
                 if index == 0 and step in EARLY:
                     runs = column_runs(EARLY[step], 512)
-                    scalar_queue.extend([(ln, run) for run in runs] + [(tanh, run) for run in runs])
-                if index in (0, 2) and scalar_queue:
-                    work_item, run = scalar_queue.pop(0)
-                    work_item(run)
-                    if work_item is tanh:
-                        vector_queue.append((times_z, run))
-                    elif scalar_queue[0][0] is tanh:
-                        for s in held:
-                            sigmoid(s)
-                        held.clear()
-                if index == 1 and 0 <= step + 1 < n_slots:
+                    if EARLY[step][0] in ARS_EARLY:
+                        scalar_queue.extend([(rsqrt, run) for run in runs])
+                    else:
+                        scalar_queue.extend([(ln, run) for run in runs] + [(tanh, run) for run in runs])
+                if index in SP and scalar_queue:
+                    run_scalar()
+                if index == 1 and 0 <= step + 1 < n_slots and step + 1 not in codes:
                     codes[step + 1] = quantise_slot(step + 1)
+            if step == -2:
+                for half in range(2):
+                    words_of = words_of_rows(rf_raw[half])
+                    transpose_bank(lambda c, j, u: words_of(c % 2, j, u), 1, half, x_grouped[0][:], "VS"[half])
+            if not MXFIRST:
+                mean_part(len(mean_queue))
+            for s in range(n_slots):
+                if s - lag(s) == step and s not in acc and s in codes and not (s == N_FIRST and step == N_FIRST - 1):
+                    acc[s] = multiply_slot(s)
+            if step == N_FIRST - 3 and DRAIN:
+                mean_part(len(mean_queue))
+                codes[N_FIRST - 1] = quantise_slot(N_FIRST - 1)
+                acc[N_FIRST - 1] = multiply_slot(N_FIRST - 1)
             mean_part(len(mean_queue))
-            if 0 <= step < n_slots:
-                acc[step] = multiply_slot(step)
             if step == N_FIRST - 2:
                 nc.vector.tensor_copy(out=mean_columns[:, :BANK], in_=mean_banks[0][:])
                 nc.scalar.copy(out=mean_columns[:, BANK:], in_=mean_banks[1][:])
@@ -339,18 +459,23 @@ def tile_gnn_layer_pa_kernel(tc, BB_feature, RF_feature, W_rfrf, b_rfrf, W_bbrf,
                 progress.add("mean_done")
                 transpose_bank(words_of_rows(mean_rows), 1, 0, x_grouped[1][:], "V")
                 quantise_x(1)
+                if LAGB:
+                    acc[N_FIRST] = multiply_slot(N_FIRST)
 
-        late_runs = column_runs(LATE, 512)
-        for run in late_runs:
-            ln(run)
-        for run in late_runs:
-            tanh(run)
-        for s in LAST:
-            finish_by_reciprocal(s)
+        while scalar_queue:
+            run_scalar()
+        late_runs = column_runs(LATE, CHL)
+        for i, run in enumerate(late_runs):
+            rsqrt(run)
+            if POSTSQ and SQ[i % len(SQ)] == "S":
+                squared(run, "S")
         for work_item, run in vector_queue:
-            work_item(run)
-        for i in range(len(late_runs) + 1):
-            if i < len(late_runs):
-                times_z(late_runs[i])
-            if i > 0:
-                add_and_store(late_runs[i - 1].start - D_RF, late_runs[i - 1].stop - D_RF)
+            product(work_item, run)
+        sums(0)
+        for i, run in enumerate(late_runs):
+            if POSTSQ and SQ[i % len(SQ)] == "V":
+                squared(run, "V")
+            before = len(ready)
+            product(less_one_times_z, run)
+            sums(len(ready) - before)
+        sums(0)

@@ -18,7 +18,7 @@ K_PASS = 512
 LN_FLOOR = 1e-30
 BANK = 512
 
-N_FIRST = 2
+N_FIRST = 3
 LAYER0 = [(0, 256 * i, 2) for i in range(7)] + [(0, 1792, 1), (0, 1920, 1)]
 SLOTS = LAYER0[:N_FIRST] + [(1, 512 * i, 4) for i in range(4)] + LAYER0[N_FIRST:]
 EARLY = {8: range(0, 7)}
@@ -30,9 +30,9 @@ GCH = 256
 SQ1 = "S"
 SQ1LAST = "S"
 LAGN = 1
-ORD = "VV.."
-ORDFROM = 4
-ORDTO = 7
+ORD = "..G."
+ORDFROM = 2
+ORDTO = 10
 POSTSQ = 1
 SUMB = 1
 SQ = "S"
@@ -49,8 +49,8 @@ VSTOP = 9
 BBE = 0
 MB = 0
 
-COPIES = "SSSS"
-COPIES_BESIDE_LN = "SSSS"
+COPIES = "VSSS"
+COPIES_BESIDE_LN = "VSSV"
 FLOPS = 2 * P * D_RF * (D_RF + D_BB)
 
 
@@ -168,18 +168,19 @@ def tile_gnn_layer_pa_kernel(tc, BB_feature, RF_feature, W_rfrf, b_rfrf, W_bbrf,
         def order_words(s, index, engine):
             j_rows = SLOTS[s][2]
             if s not in ordered:
-                ordered[s] = [work.tile([P, 4, BANK], F32, tag="ordered", name="ordered"), set()]
-            passes = DEPTH[SLOTS[s][0]] // K_PASS // len(w_raw[s])
-            words_raw = lambda c: w_raw[s][c // passes][:].rearrange("p j k -> p (j k)").bitcast(F32).rearrange("p (j c w u) -> p c j u w", j=j_rows, c=passes, u=2)[:, c % passes, :, :, :]
+                ordered[s] = [work.tile([P, 4, BANK], U32, tag="ordered", name="ordered"), set()]
             ordered[s][1].add(index)
+            word = U32 if engine == "G" else F32
+            passes = DEPTH[SLOTS[s][0]] // K_PASS
+            words = w_raw[s][0][:].rearrange("p j k -> p (j k)").bitcast(word)
+            words = words.rearrange("p (j c w u) -> p c j u w", j=j_rows, c=passes, u=2)
             c, j = divmod(2 * index, j_rows)
             if j_rows == 1:
-                words = w_raw[s][0][:].rearrange("p j k -> p (j k)").bitcast(F32).rearrange("p (c w u) -> p c u w", c=passes, u=2)[:, c : c + 2, :, :]
+                words = words[:, c : c + 2, 0, :, :]
             else:
-                words = words_raw(c)[:, j : j + 2, :, :]
+                words = words[:, c, j : j + 2, :, :]
             copy_on(engine)(
-                out=ordered[s][0][:, index, :].rearrange("p (h u w) -> p h u w", h=2, u=2),
-                in_=words,
+                out=ordered[s][0][:, index, :].bitcast(word).rearrange("p (h u w) -> p h u w", h=2, u=2), in_=words
             )
 
         def words_of_slot(s):
@@ -189,7 +190,7 @@ def tile_gnn_layer_pa_kernel(tc, BB_feature, RF_feature, W_rfrf, b_rfrf, W_bbrf,
             def words_of(c, j, u):
                 index, h = divmod(c * SLOTS[s][2] + j, 2)
                 if s in ordered and index in ordered[s][1]:
-                    return ordered[s][0][:, index, (2 * h + u) * P : (2 * h + u + 1) * P]
+                    return ordered[s][0][:, index, (2 * h + u) * P : (2 * h + u + 1) * P].bitcast(F32)
                 words = w_raw[s][c // passes][:, j, :].bitcast(F32)
                 c_in = c % passes
                 return words[:, 256 * c_in + u : 256 * c_in + 256 : 2]
@@ -247,6 +248,11 @@ def tile_gnn_layer_pa_kernel(tc, BB_feature, RF_feature, W_rfrf, b_rfrf, W_bbrf,
             columns = columns_of(s)
             nc.scalar.activation(out=q[:, columns], in_=z[:, columns], func=ACT.Sigmoid, scale=-1.0)
             if s in LATE or s in ARS_EARLY:
+                squares.append(s)
+
+        def square(s):
+            columns = columns_of(s)
+            if True:
                 sq = SQ1LAST if s >= 10 else SQ1
                 if sq == "S":
                     nc.scalar.activation(out=q[:, columns], in_=q[:, columns], func=ACT.Square)
@@ -270,6 +276,8 @@ def tile_gnn_layer_pa_kernel(tc, BB_feature, RF_feature, W_rfrf, b_rfrf, W_bbrf,
                 for a in range(columns.start, columns.stop, GCH):
                     part = slice(a, min(a + GCH, columns.stop))
                     nc.gpsimd.tensor_tensor(out=q[:, part], in0=z[:, part], in1=q[:, part], op=ALU.mult)
+
+        squares = []
 
         def rsqrt(columns):
             nc.scalar.activation(
@@ -422,6 +430,8 @@ def tile_gnn_layer_pa_kernel(tc, BB_feature, RF_feature, W_rfrf, b_rfrf, W_bbrf,
                     product(work_item, run)
                 if index == 2 and SUMB and step < VSTOP:
                     sums(0)
+                if squares:
+                    square(squares.pop(0))
                 for s in range(n_slots):
                     if index == SIGI and s + 1 + SIGD - lag(s) == step:
                         if scalar_queue and scalar_queue[0][0] is not tanh:
@@ -464,11 +474,16 @@ def tile_gnn_layer_pa_kernel(tc, BB_feature, RF_feature, W_rfrf, b_rfrf, W_bbrf,
 
         while scalar_queue:
             run_scalar()
+        while squares:
+            square(squares.pop(0))
         late_runs = column_runs(LATE, CHL)
+        on_scalar = [run for i, run in enumerate(late_runs) if POSTSQ and SQ[i % len(SQ)] == "S"]
         for i, run in enumerate(late_runs):
             rsqrt(run)
-            if POSTSQ and SQ[i % len(SQ)] == "S":
-                squared(run, "S")
+            if i and late_runs[i - 1] in on_scalar:
+                squared(late_runs[i - 1], "S")
+        if late_runs[-1] in on_scalar:
+            squared(late_runs[-1], "S")
         for work_item, run in vector_queue:
             product(work_item, run)
         sums(0)

import concourse.mybir as mybir
from concourse.masks import make_identity

F32 = mybir.dt.float32
BF16 = mybir.dt.bfloat16
U32 = mybir.dt.uint32
U8 = mybir.dt.uint8
FP8X4 = mybir.dt.float8_e4m3fn_x4
ACT = mybir.ActivationFunctionType
ALU = mybir.AluOpType

P = 128
GROUPS = 16
D_BB = 1024
D_RF = 2048
DEPTH = (D_RF, D_BB)
K_PASS = 512
LN_FLOOR = 1e-30
BANK = 512

N_FIRST = 3
LAYER0 = [(0, 256 * i, 2) for i in range(7)] + [(0, 1792, 1), (0, 1920, 1)]
SLOTS = LAYER0[:N_FIRST] + [(1, 512 * i, 4) for i in range(4)] + LAYER0[N_FIRST:]
EARLY = {8: range(0, 7)}
LATE = range(7, 13)
COPIES_LATE = "VVVV"
LATEFROM = 9
PROD = "V"
GCH = 256
SQ1 = "S"
SQ1LAST = "S"
LAGN = 1
ORD = "..G."
ORDFROM = 2
ORDTO = 10
POSTSQ = 1
SUMB = 1
SQ = "S"
DRAIN = 0
LAGB = 0
SIGD = 0
SIGI = 2
MXFIRST = 0
SP = (0,1,2,3)
CHL = 256
SQ2 = "S"
ARS_EARLY = ()
VSTOP = 9
BBE = 0
MB = 0

COPIES = "VSSS"
COPIES_BESIDE_LN = "VSSV"
FLOPS = 2 * P * D_RF * (D_RF + D_BB)


def tile_gnn_layer_pa_kernel(tc, BB_feature, RF_feature, W_rfrf, b_rfrf, W_bbrf, b_bbrf, out):
    nc = tc.nc
    n_slots = len(SLOTS)
    with (
        tc.tile_pool(name="const", bufs=1) as const,
        tc.tile_pool(name="work", bufs=2) as work,
        tc.psum_pool(name="tp", bufs=4) as tp,
        tc.psum_pool(name="accp", bufs=2) as accp,
        tc.psum_pool(name="meanp", bufs=1) as meanp,
        tc.manual_schedule(),
    ):
        bias_rows = const.tile([P, P], BF16)
        nc.gpsimd.memset(bias_rows[:], 0.0)
        nc.sync.dma_start(out=bias_rows[0:16, :], in_=b_rfrf.rearrange("(r c) -> r c", c=P))
        nc.sync.dma_start(out=bias_rows[16:32, :], in_=b_bbrf.rearrange("(r c) -> r c", c=P))

        w_raw = {}

        def load_slot(s, pieces):
            layer, first, j_rows = SLOTS[s]
            rows = (W_rfrf, W_bbrf)[layer][first : first + P * j_rows, :].rearrange("(n j) k -> n j k", j=j_rows)
            width = DEPTH[layer] // pieces
            w_raw[s] = []
            for i in range(pieces):
                raw = const.tile([P, j_rows, width], BF16, name="w_raw_%d_%d" % (s, i))
                nc.sync.dma_start(out=raw[:], in_=rows[:, :, i * width : (i + 1) * width])
                w_raw[s].append(raw)

        bb_raw = []

        def load_bb(i):
            raw = const.tile([P, 4 * D_BB], BF16, name="bb_raw_%d" % i)
            rows = BB_feature.rearrange("b g d -> (b g) d")[i * 512 : (i + 1) * 512, :]
            nc.sync.dma_start(out=raw[:], in_=rows.rearrange("(p e) d -> p (e d)", e=4))
            bb_raw.append(raw)

        load_slot(0, 2)
        rf_raw = []
        for half in range(2):
            raw = const.tile([P, D_RF // 2], BF16, name="rf_raw_%d" % half)
            nc.sync.dma_start(out=raw[:], in_=RF_feature[:, half * D_RF // 2 : (half + 1) * D_RF // 2])
            rf_raw.append(raw)
        for s in range(1, n_slots):
            load_slot(s, 1)
            if s == N_FIRST - 1 - BBE:
                load_bb(0)
                load_bb(1)
            if s == N_FIRST - BBE:
                load_bb(2)
                load_bb(3)

        scratch = const.tile([P, 1], F32)
        nc.vector.memset(scratch[:], 0.0)
        nc.scalar.activation(out=scratch[:], in_=scratch[:], func=ACT.Sigmoid)
        ident = const.tile([P, P], F32)
        make_identity(nc, ident[:])
        ident_bf16 = const.tile([P, P], BF16)
        nc.vector.tensor_copy(out=ident_bf16[:], in_=ident[:])
        sel_f32 = const.tile([P, 32], F32)
        nc.vector.tensor_reduce(
            out=sel_f32[:],
            in_=ident[:].rearrange("p (n i) -> p n i", i=4),
            axis=mybir.AxisListType.X,
            op=ALU.add,
        )
        sel = const.tile([P, 32], BF16)
        nc.vector.tensor_scalar(out=sel[:], in0=sel_f32[:], scalar1=1.0 / GROUPS, scalar2=None, op0=ALU.mult)

        z = const.tile([P, 2 * D_RF], F32)
        q = const.tile([P, 2 * D_RF], F32)
        bias = const.tile([P, 2 * D_RF], BF16)
        x_grouped = [const.tile([P, k], BF16, align_bytes=64, name="x_grouped_%d" % k) for k in DEPTH]
        x_codes = [const.tile([P, k // 4], U32, align_bytes=64, name="x_codes_%d" % k) for k in DEPTH]
        x_scales = [const.tile([P, k // 4], U8, align_bytes=64, name="x_scales_%d" % k) for k in DEPTH]
        mean_banks = [meanp.tile([P, BANK], F32, tag="mean%d" % c, name="mean%d" % c) for c in range(2)]
        mean_columns = const.tile([P, D_BB], BF16)
        mean_rows = const.tile([P, D_BB], BF16)

        banks_used = []

        def next_bank():
            turn = len(banks_used)
            banks_used.append(turn)
            if "mean_done" in progress and turn % 6 >= 4:
                return meanp.tile([P, BANK], F32, tag="mean%d" % (turn % 6 - 4), name="late_bank")
            return tp.tile([P, BANK], F32, tag="tp", name="bank")

        progress = set()

        def copy_on(engine):
            return {"V": nc.vector.tensor_copy, "S": nc.scalar.copy, "G": nc.gpsimd.tensor_copy}[engine]

        def transpose_bank(words_of, j_rows, index, grouped, engine):
            bank = next_bank()
            for h in range(2):
                c, j = divmod(2 * index + h, j_rows)
                for u in range(2):
                    columns = slice((2 * h + u) * P, (2 * h + u + 1) * P)
                    nc.tensor.transpose(bank[:, columns], words_of(c, j, u), ident[:])
            words = grouped.bitcast(F32).rearrange("p (g n u) -> p g n u", n=P, u=2)
            copy_on(engine)(
                out=words[:, 2 * index : 2 * index + 2, :, :],
                in_=bank[:].rearrange("p (h u n) -> p h n u", h=2, u=2),
            )

        def words_of_rows(tile):
            words = tile[:].bitcast(F32)
            return lambda c, j, u: words[:, 256 * c + u : 256 * c + 256 : 2]

        ordered = {}

        def order_words(s, index, engine):
            j_rows = SLOTS[s][2]
            if s not in ordered:
                ordered[s] = [work.tile([P, 4, BANK], U32, tag="ordered", name="ordered"), set()]
            ordered[s][1].add(index)
            word = U32 if engine == "G" else F32
            passes = DEPTH[SLOTS[s][0]] // K_PASS
            words = w_raw[s][0][:].rearrange("p j k -> p (j k)").bitcast(word)
            words = words.rearrange("p (j c w u) -> p c j u w", j=j_rows, c=passes, u=2)
            c, j = divmod(2 * index, j_rows)
            if j_rows == 1:
                words = words[:, c : c + 2, 0, :, :]
            else:
                words = words[:, c, j : j + 2, :, :]
            copy_on(engine)(
                out=ordered[s][0][:, index, :].bitcast(word).rearrange("p (h u w) -> p h u w", h=2, u=2), in_=words
            )

        def words_of_slot(s):
            layer = SLOTS[s][0]
            passes = DEPTH[layer] // K_PASS // len(w_raw[s])

            def words_of(c, j, u):
                index, h = divmod(c * SLOTS[s][2] + j, 2)
                if s in ordered and index in ordered[s][1]:
                    return ordered[s][0][:, index, (2 * h + u) * P : (2 * h + u + 1) * P].bitcast(F32)
                words = w_raw[s][c // passes][:, j, :].bitcast(F32)
                c_in = c % passes
                return words[:, 256 * c_in + u : 256 * c_in + 256 : 2]

            return words_of

        def columns_of(s):
            layer, first, j_rows = SLOTS[s]
            return slice(layer * D_RF + first, layer * D_RF + first + P * j_rows)

        def quantise_x(layer):
            nc.vector.quantize_mx(
                out=x_codes[layer][:].bitcast(FP8X4), scales=x_scales[layer][:], in_=x_grouped[layer][:]
            )

        def quantise_slot(s):
            layer, first, j_rows = SLOTS[s]
            n_words = j_rows * DEPTH[layer] // 4
            codes = work.tile([P, 1024], U32, align_bytes=64, tag="codes", name="codes")
            scales = work.tile([P, 1024], U8, align_bytes=64, tag="scales", name="scales")
            nc.vector.quantize_mx(
                out=codes[:, :n_words].bitcast(FP8X4), scales=scales[:, :n_words], in_=grouped[s][:, : 4 * n_words]
            )
            return codes, scales

        def multiply_slot(s):
            layer, first, j_rows = SLOTS[s]
            width = P * j_rows
            passes = DEPTH[layer] // K_PASS
            w_codes, w_scales = codes[s]
            result = accp.tile([P, BANK], F32, tag="acc", name="acc")
            for c in range(passes):
                nc.tensor.matmul_mx(
                    out=result[:, :width],
                    lhsT=x_codes[layer][:, c * P : (c + 1) * P].bitcast(FP8X4),
                    lhsT_scale=x_scales[layer][:, c * P : (c + 1) * P],
                    rhs=w_codes[:, c * width : (c + 1) * width].bitcast(FP8X4),
                    rhs_scale=w_scales[:, c * width : (c + 1) * width],
                    start=(c == 0),
                    stop=(c == passes - 1),
                )
            return result

        def add_bias(s):
            j_rows = SLOTS[s][2]
            columns = columns_of(s)
            nc.vector.tensor_tensor(
                out=z[:, columns].rearrange("p (n j) -> p n j", j=j_rows),
                in0=acc[s][:, : P * j_rows].rearrange("p (j n) -> p n j", j=j_rows),
                in1=bias[:, columns].rearrange("p (n j) -> p n j", j=j_rows),
                op=ALU.add,
            )

        def sigmoid(s):
            columns = columns_of(s)
            nc.scalar.activation(out=q[:, columns], in_=z[:, columns], func=ACT.Sigmoid, scale=-1.0)
            if s in LATE or s in ARS_EARLY:
                squares.append(s)

        def square(s):
            columns = columns_of(s)
            if True:
                sq = SQ1LAST if s >= 10 else SQ1
                if sq == "S":
                    nc.scalar.activation(out=q[:, columns], in_=q[:, columns], func=ACT.Square)
                elif sq == "V":
                    nc.vector.tensor_tensor(out=q[:, columns], in0=q[:, columns], in1=q[:, columns], op=ALU.mult)
                else:
                    nc.gpsimd.tensor_tensor(out=q[:, columns], in0=q[:, columns], in1=q[:, columns], op=ALU.mult)
                if SQ2 == "S" and not POSTSQ:
                    nc.scalar.activation(out=q[:, columns], in_=q[:, columns], func=ACT.Square, bias=1.0)

        def ln(columns):
            nc.scalar.activation(out=q[:, columns], in_=q[:, columns], func=ACT.Ln, bias=LN_FLOOR)

        def tanh(columns):
            nc.scalar.activation(out=q[:, columns], in_=q[:, columns], func=ACT.Tanh, scale=-1.0)

        def times_z(columns):
            if PROD == "V":
                nc.vector.tensor_tensor(out=q[:, columns], in0=z[:, columns], in1=q[:, columns], op=ALU.mult)
            else:
                for a in range(columns.start, columns.stop, GCH):
                    part = slice(a, min(a + GCH, columns.stop))
                    nc.gpsimd.tensor_tensor(out=q[:, part], in0=z[:, part], in1=q[:, part], op=ALU.mult)

        squares = []

        def rsqrt(columns):
            nc.scalar.activation(
                out=q[:, columns], in_=q[:, columns], func=ACT.Abs_reciprocal_sqrt, scale=0.5 if POSTSQ else 0.25, bias=0.5 if POSTSQ else 0.0
            )

        def squared(columns, engine):
            if engine == "S":
                nc.scalar.activation(out=q[:, columns], in_=q[:, columns], func=ACT.Square)
            else:
                nc.vector.tensor_tensor(out=q[:, columns], in0=q[:, columns], in1=q[:, columns], op=ALU.mult)

        def less_one_times_z(columns):
            part = q[:, columns]
            nc.vector.scalar_tensor_tensor(
                out=part, in0=part, scalar=-1.0, in1=z[:, columns], op0=ALU.add, op1=ALU.mult
            )

        def add_and_store(first, last):
            nc.vector.tensor_tensor(
                out=z[:, first:last], in0=q[:, first:last], in1=q[:, D_RF + first : D_RF + last], op=ALU.add
            )
            nc.sync.dma_start(out=out[:, first:last], in_=z[:, first:last])

        def column_runs(slots, longest):
            runs = []
            for s in slots:
                columns = columns_of(s)
                if runs and runs[-1].stop == columns.start and columns.stop - runs[-1].start <= longest:
                    runs[-1] = slice(runs[-1].start, columns.stop)
                else:
                    runs.append(columns)
            return runs

        bias_columns = const.tile([P, 32], BF16)

        def turn_biases():
            bank = tp.tile([P, P], BF16, tag="tp", name="bias_turn")
            nc.tensor.transpose(bank[:], bias_rows[:], ident_bf16[:])
            nc.vector.tensor_copy(out=bias_columns[:], in_=bank[:, :32])

        def spread_biases(index, engine):
            bank = tp.tile([P, 1024], BF16, tag="tp", name="bias_bank")
            for i in range(8):
                r = 8 * index + i
                nc.tensor.transpose(
                    bank[:, i * P : (i + 1) * P], bias_columns[:, r : r + 1].to_broadcast([P, P]), ident_bf16[:]
                )
            copy_on(engine)(out=bias[:, index * 1024 : (index + 1) * 1024], in_=bank[:])

        mean_queue = []

        def mean_part(n):
            for unused in range(min(n, len(mean_queue))):
                i, h = mean_queue.pop(0)
                rows = bb_raw[i][:].rearrange("p (e d) -> p e d", e=4)
                place = (h % 4) * P + 32 * i
                for e in range(4):
                    nc.tensor.matmul(
                        out=mean_banks[h // 4][:, place : place + 32],
                        lhsT=rows[:, e, h * P : (h + 1) * P],
                        rhs=sel[:],
                        start=(e == 0),
                        stop=(e == 3),
                    )

        grouped = {}
        codes = {}
        acc = {}
        scalar_queue = []
        vector_queue = []
        held = []

        finished = set()
        ready = []

        def product(work_item, run):
            work_item(run)
            for a in range(run.start, run.stop, P):
                finished.add(a)
                if (a + D_RF) % (2 * D_RF) in finished:
                    ready.append(a % D_RF)

        def sums(keep):
            blocks = sorted(ready[: len(ready) - keep])
            rest = ready[len(ready) - keep :]
            ready.clear()
            ready.extend(rest)
            while blocks:
                n = 1
                while n < len(blocks) and n < 6 and blocks[n] == blocks[0] + n * P:
                    n += 1
                add_and_store(blocks[0], blocks[0] + n * P)
                blocks = blocks[n:]

        def run_scalar():
            work_item, run = scalar_queue.pop(0)
            work_item(run)
            if work_item is tanh:
                vector_queue.append((times_z, run))
            elif work_item is rsqrt:
                vector_queue.append((less_one_times_z, run))
            if not scalar_queue or (work_item is ln and scalar_queue[0][0] is tanh):
                for s in held:
                    sigmoid(s)
                held.clear()

        turn_biases()
        for index in range(4):
            spread_biases(index, "VS"[index % 2])
        def lag(s):
            if DRAIN and s == N_FIRST - 1:
                return 2
            return LAGN if s < N_FIRST else LAGB

        for step in range(-2, n_slots + 2):
            t = step + 2
            n_banks = 0
            if t < n_slots:
                layer, first, j_rows = SLOTS[t]
                n_banks = j_rows * DEPTH[layer] // 1024
                grouped[t] = work.tile([P, 4096], BF16, align_bytes=64, tag="grouped", name="grouped", bufs=3)
            if step == N_FIRST - 3:
                mean_queue.extend([(i, h) for i in range(2) for h in range(8)])
            if step == N_FIRST - 2:
                mean_queue.extend([(i, h) for i in range(2, 4) for h in range(8)])
            if step == -1:
                quantise_x(0)
            for s in range(n_slots):
                if s + 1 - lag(s) == step:
                    add_bias(s)
            if step == N_FIRST - 1:
                rows_bank = tp.tile([P, D_BB], BF16, tag="tp", name="rows_bank")
                for h in range(8):
                    columns = slice(h * P, (h + 1) * P)
                    nc.tensor.transpose(rows_bank[:, columns], mean_columns[:, columns], ident_bf16[:])
                nc.scalar.copy(out=mean_rows[:], in_=rows_bank[:])
            engines = COPIES_BESIDE_LN if scalar_queue or step in EARLY else COPIES
            if t >= LATEFROM:
                engines = COPIES_LATE
            for index in range(4):
                if ORDFROM <= t + 1 < min(n_slots, ORDTO) and index < SLOTS[t + 1][2] * DEPTH[SLOTS[t + 1][0]] // 1024 and ORD[index] != ".":
                    order_words(t + 1, index, ORD[index])
                if index < n_banks:
                    transpose_bank(words_of_slot(t), j_rows, index, grouped[t][:, : 1024 * n_banks], engines[index])
                if index:
                    mean_part(MB)
                if index == 0 and vector_queue and step < VSTOP:
                    work_item, run = vector_queue.pop(0)
                    product(work_item, run)
                if index == 2 and SUMB and step < VSTOP:
                    sums(0)
                if squares:
                    square(squares.pop(0))
                for s in range(n_slots):
                    if index == SIGI and s + 1 + SIGD - lag(s) == step:
                        if scalar_queue and scalar_queue[0][0] is not tanh:
                            held.append(s)
                        else:
                            sigmoid(s)
                if index == 0 and step in EARLY:
                    runs = column_runs(EARLY[step], 512)
                    if EARLY[step][0] in ARS_EARLY:
                        scalar_queue.extend([(rsqrt, run) for run in runs])
                    else:
                        scalar_queue.extend([(ln, run) for run in runs] + [(tanh, run) for run in runs])
                if index in SP and scalar_queue:
                    run_scalar()
                if index == 1 and 0 <= step + 1 < n_slots and step + 1 not in codes:
                    codes[step + 1] = quantise_slot(step + 1)
            if step == -2:
                for half in range(2):
                    words_of = words_of_rows(rf_raw[half])
                    transpose_bank(lambda c, j, u: words_of(c % 2, j, u), 1, half, x_grouped[0][:], "VS"[half])
            if not MXFIRST:
                mean_part(len(mean_queue))
            for s in range(n_slots):
                if s - lag(s) == step and s not in acc and s in codes and not (s == N_FIRST and step == N_FIRST - 1):
                    acc[s] = multiply_slot(s)
            if step == N_FIRST - 3 and DRAIN:
                mean_part(len(mean_queue))
                codes[N_FIRST - 1] = quantise_slot(N_FIRST - 1)
                acc[N_FIRST - 1] = multiply_slot(N_FIRST - 1)
            mean_part(len(mean_queue))
            if step == N_FIRST - 2:
                nc.vector.tensor_copy(out=mean_columns[:, :BANK], in_=mean_banks[0][:])
                nc.scalar.copy(out=mean_columns[:, BANK:], in_=mean_banks[1][:])
            if step == N_FIRST - 1:
                progress.add("mean_done")
                transpose_bank(words_of_rows(mean_rows), 1, 0, x_grouped[1][:], "V")
                quantise_x(1)
                if LAGB:
                    acc[N_FIRST] = multiply_slot(N_FIRST)

        while scalar_queue:
            run_scalar()
        while squares:
            square(squares.pop(0))
        late_runs = column_runs(LATE, CHL)
        on_scalar = [run for i, run in enumerate(late_runs) if POSTSQ and SQ[i % len(SQ)] == "S"]
        for i, run in enumerate(late_runs):
            rsqrt(run)
            if i and late_runs[i - 1] in on_scalar:
                squared(late_runs[i - 1], "S")
        if late_runs[-1] in on_scalar:
            squared(late_runs[-1], "S")
        for work_item, run in vector_queue:
            product(work_item, run)
        sums(0)
        for i, run in enumerate(late_runs):
            if POSTSQ and SQ[i % len(SQ)] == "V":
                squared(run, "V")
            before = len(ready)
            product(less_one_times_z, run)
            sums(len(ready) - before)
        sums(0)
